import numpy as np
import ml_dtypes


def mxq(x, axis, fmt="e4m3"):
    dtype, down = {"e4m3": (ml_dtypes.float8_e4m3fn, 7), "e5m2": (ml_dtypes.float8_e5m2, 14)}[fmt]
    v = np.moveaxis(np.asarray(x, np.float32).astype(ml_dtypes.bfloat16).astype(np.float64), axis, -1)
    blocks = v.reshape(v.shape[:-1] + (-1, 32))
    amax = np.abs(blocks).max(-1, keepdims=True)
    byte = np.maximum(np.where(amax > 0, np.frexp(amax)[1] - 1 + 127, 0) - down, 1)
    scale = np.exp2(byte - 127.0)
    codes = (blocks / scale).astype(np.float32).astype(dtype).astype(np.float64)
    return np.moveaxis((codes * scale).reshape(v.shape), -1, axis)


WIDE = False


def mx_kscale(k):
    if not WIDE:
        return np.ones(k)
    levels = np.array([10, -10, 5, -5, 0])
    a = np.random.permutation(np.resize(levels, k // 512 * 4)).reshape(k // 512, 4)
    idx = np.arange(k)
    return np.exp2(a[idx // 512, idx % 128 // 32])


BF16 = ml_dtypes.bfloat16


def bf(x):
    return np.asarray(x, np.float32).astype(BF16)


def f64(x):
    return np.asarray(x).astype(np.float64)


E2M1 = np.array([0.0, 0.5, 1.0, 1.5, 2.0, 3.0, 4.0, 6.0, -0.0, -0.5, -1.0, -1.5, -2.0, -3.0, -4.0, -6.0])


def pack_weight(w, fmt):
    k, n = w.shape
    w = f64(bf(w)).reshape(k // 32, 32, n)
    amax = np.abs(w).max(1)
    if fmt == "e4m3":
        byte = np.frexp(amax)[1] - 1 + 127 - 7
    else:
        mant, ex = np.frexp(amax / 6.0)
        byte = np.where(mant > 0.5, ex, ex - 1) + 127
    byte = np.clip(np.where(amax > 0, byte, 1), 1, 254)
    scaled = (w * np.exp2(127.0 - byte)[:, None, :]).reshape(k, n).astype(np.float32)
    by_word = np.ascontiguousarray(scaled.reshape(k // 512, 128, 4, n).transpose(0, 1, 3, 2))
    if fmt == "e4m3":
        words = by_word.astype(ml_dtypes.float8_e4m3fn).view(np.uint8)
    else:
        c = by_word.astype(ml_dtypes.float4_e2m1fn).view(np.uint8) & 0xF
        words = c[..., 0::2] | (c[..., 1::2] << 4)
    return np.ascontiguousarray(words), np.ascontiguousarray(byte.astype(np.uint8).reshape(k // 512, 16, n))


def unpack_weight(words, scales, fmt):
    g, p, n, _ = words.shape
    if fmt == "e4m3":
        vals = np.ascontiguousarray(words).view(ml_dtypes.float8_e4m3fn).astype(np.float64)
    else:
        nib = np.empty((g, p, n, 4), np.uint8)
        nib[..., 0::2] = words & 0xF
        nib[..., 1::2] = words >> 4
        vals = E2M1[nib]
    vals = vals * np.repeat(np.exp2(scales.astype(np.float64) - 127.0), 8, axis=1)[..., None]
    return vals.transpose(0, 1, 3, 2).reshape(g * 512, n)


B, S, D, H, HD, M, G = 4, 128, 1024, 8, 128, 4096, 3
EPS = 1e-6
HH = H * HD
FMT = "e4m3"


def silu(v):
    return v / (1.0 + np.exp(-v))


def rmsnorm(x, gain):
    var = np.mean(np.square(x), axis=-1, keepdims=True)
    return x * (1.0 / np.sqrt(var + EPS)) * gain


def setup_inputs():
    s, t = mx_kscale(HH), mx_kscale(D)
    attn = bf(0.3 * np.random.standard_normal((B, S, HH)) * s)
    x = bf(np.random.standard_normal((B, S, D)))
    w_o_words, w_o_scales = pack_weight(np.random.standard_normal((HH, D)) * 2.0 / np.sqrt(HH) / s[:, None], FMT)
    rms2_scale = bf((1.0 + 0.1 * np.random.standard_normal(D)) * t)
    w_gate_words, w_gate_scales = pack_weight(np.random.standard_normal((D, M)) / np.sqrt(D) / t[:, None], FMT)
    w_up_words, w_up_scales = pack_weight(np.random.standard_normal((D, M)) / np.sqrt(D) / t[:, None], FMT)
    return {"attn": attn,
            "x": x,
            "w_o_words": w_o_words,
            "w_o_scales": w_o_scales,
            "rms2_scale": rms2_scale,
            "w_gate_words": w_gate_words,
            "w_gate_scales": w_gate_scales,
            "w_up_words": w_up_words,
            "w_up_scales": w_up_scales}


def reference(attn, x, w_o_words, w_o_scales, rms2_scale, w_gate_words, w_gate_scales, w_up_words, w_up_scales):
    x_mid = f64(x) + (mxq(f64(attn), 2, "e4m3") @ unpack_weight(w_o_words, w_o_scales, FMT))
    hq = mxq(rmsnorm(x_mid, f64(rms2_scale)), 2, "e4m3")
    g = silu(hq @ unpack_weight(w_gate_words, w_gate_scales, FMT)) * (hq @ unpack_weight(w_up_words, w_up_scales, FMT))
    return x_mid, g

@@ -1,0 +1,209 @@
+from contextlib import ExitStack
+
+import concourse.mybir as mybir
+from concourse.masks import make_identity
+
+F32 = mybir.dt.float32
+BF16 = mybir.dt.bfloat16
+I32 = mybir.dt.int32
+U32 = mybir.dt.uint32
+U8 = mybir.dt.uint8
+FP8X4 = mybir.dt.float8_e4m3fn_x4
+ALU = mybir.AluOpType
+ACT = mybir.ActivationFunctionType
+
+P = 128
+TILES = 4
+D = 1024
+M = 4096
+PASSES = D // 512
+BANK = 512
+CHUNKS = M // BANK
+STORE_CHUNKS = 2
+EPS = 1e-6
+
+FLOPS = 2 * TILES * P * D * (D + 2 * M)
+
+
+def tile_transformerblocktpu_pb_kernel(
+    tc, attn, x, w_o_words, w_o_scales, rms2_scale, w_gate_words, w_gate_scales, w_up_words, w_up_scales, out_0, out_1
+):
+    nc = tc.nc
+    with ExitStack() as ctx:
+        keep = ctx.enter_context(tc.tile_pool(name="keep", bufs=1))
+        stage = ctx.enter_context(tc.tile_pool(name="stage", bufs=2))
+        silus = ctx.enter_context(tc.tile_pool(name="silus", bufs=4))
+        psum = ctx.enter_context(tc.psum_pool(name="psum", bufs=8))
+
+        wo_planes = keep.tile([P, D], U8, align_bytes=64)
+        w_planes = keep.tile([P, M], U8, align_bytes=64)
+        gain_row = keep.tile([P, D], BF16)
+        ones = keep.tile([P, P], BF16)
+        minus_half = keep.tile([P, 1], F32)
+        ident = keep.tile([P, P], F32)
+        nc.vector.memset(wo_planes[:].bitcast(I32), 0)
+        nc.vector.memset(gain_row[:], 0.0)
+        nc.vector.memset(w_planes[:].bitcast(I32), 0)
+        nc.vector.memset(ones[:], 1.0)
+        nc.vector.memset(minus_half[:], -0.5)
+        make_identity(nc, ident[:])
+
+        attn_sb = []
+        for m in range(TILES):
+            t = keep.tile([P, D], BF16, name="attn%d" % m)
+            nc.sync.dma_start(out=t[:], in_=attn[m])
+            attn_sb.append(t)
+        for q4 in range(4):
+            nc.sync.dma_start(
+                out=wo_planes[32 * q4 : 32 * q4 + 8, :].bitcast(I32),
+                in_=w_o_scales[:, 4 * q4 : 4 * q4 + 4, :].bitcast(I32),
+            )
+        wo_words = keep.tile([P, PASSES, D], U32, align_bytes=64)
+        nc.sync.dma_start(
+            out=wo_words[:].bitcast(I32), in_=w_o_words.rearrange("g p n t -> p g (n t)").bitcast(I32)
+        )
+        nc.sync.dma_start(out=gain_row[0:1, :], in_=rms2_scale.rearrange("(o d) -> o d", o=1))
+        x_sb = []
+        for m in range(TILES):
+            t = keep.tile([P, D], BF16, name="x%d" % m)
+            nc.sync.dma_start(out=t[:], in_=x[m])
+            x_sb.append(t)
+        for w, scales in enumerate((w_gate_scales, w_up_scales)):
+            for q4 in range(4):
+                nc.sync.dma_start(
+                    out=w_planes[32 * q4 + 8 * w : 32 * q4 + 8 * w + 8, :].bitcast(I32),
+                    in_=scales[:, 4 * q4 : 4 * q4 + 4, :].bitcast(I32),
+                )
+        w_src = [wd.rearrange("g p n t -> p g (n t)").bitcast(I32) for wd in (w_gate_words, w_up_words)]
+        w_words = []
+        for c in range(CHUNKS):
+            pair = []
+            for w in range(2):
+                t = keep.tile([P, PASSES, BANK], U32, name="w%d_%d" % (w, c), align_bytes=64)
+                nc.sync.dma_start(out=t[:].bitcast(I32), in_=w_src[w][:, :, c * BANK : (c + 1) * BANK])
+                pair.append(t)
+            w_words.append(pair)
+
+        a_codes = keep.tile([P, TILES, PASSES * P], U32, align_bytes=64)
+        a_planes = keep.tile([P, TILES, PASSES * P], U8, align_bytes=64)
+        h_codes = keep.tile([P, TILES, PASSES * P], U32, align_bytes=64)
+        h_planes = keep.tile([P, TILES, PASSES * P], U8, align_bytes=64)
+        gain_bc = keep.tile([P, D], BF16)
+        x_mid = [keep.tile([P, D], F32, name="x_mid%d" % m) for m in range(TILES)]
+        g_sb = [keep.tile([P, M], F32, name="g%d" % m) for m in range(TILES)]
+        mean_sq = [keep.tile([P, 2], F32, name="mean_sq%d" % m) for m in range(TILES)]
+        var = [keep.tile([P, 1], F32, name="var%d" % m) for m in range(TILES)]
+        rstd = [keep.tile([P, 1], F32, name="rstd%d" % m) for m in range(TILES)]
+        h_sb = [keep.tile([P, D], BF16, name="h%d" % m) for m in range(TILES)]
+        s1_banks = {}
+
+        def flip_and_quantise(rows, codes, planes):
+            words = rows.bitcast(F32)
+            flipped = psum.tile([P, PASSES, 2, P], F32, tag="bank", name="flipped")
+            for g in range(PASSES):
+                for u in range(2):
+                    nc.tensor.transpose(flipped[:, g, u, :], words[:, 256 * g + u : 256 * (g + 1) : 2], ident[:])
+            grouped = stage.tile([P, PASSES * P * 4], BF16, align_bytes=64, name="grouped")
+            nc.scalar.copy(
+                out=grouped[:].bitcast(F32).rearrange("p (g r u) -> p g r u", g=PASSES, u=2),
+                in_=flipped[:].rearrange("p g u r -> p g r u"),
+            )
+            nc.vector.quantize_mx(out=codes.bitcast(FP8X4), scales=planes, in_=grouped[:])
+
+        def stage1(m):
+            for n in range(2):
+                acc = psum.tile([P, BANK], F32, tag="bank", name="acc1")
+                for g in range(PASSES):
+                    nc.tensor.matmul_mx(
+                        out=acc[:],
+                        lhsT=a_codes[:, m, g * P : (g + 1) * P].bitcast(FP8X4),
+                        lhsT_scale=a_planes[:, m, g * P : (g + 1) * P],
+                        rhs=wo_words[:, g, n * BANK : (n + 1) * BANK].bitcast(FP8X4),
+                        rhs_scale=wo_planes[4 * g : P, n * BANK : (n + 1) * BANK],
+                        start=(g == 0),
+                        stop=(g == PASSES - 1),
+                    )
+                s1_banks[(m, n)] = acc
+
+        def residual(m):
+            for n in range(2):
+                cols = slice(n * BANK, (n + 1) * BANK)
+                nc.vector.tensor_tensor(out=x_mid[m][:, cols], in0=s1_banks[(m, n)][:], in1=x_sb[m][:, cols], op=ALU.add)
+                squares = stage.tile([P, BANK], BF16, name="squares")
+                nc.scalar.activation(
+                    out=squares[:], in_=x_mid[m][:, cols], func=ACT.Square, scale=1.0 / 32.0,
+                    accum_out=mean_sq[m][:, n : n + 1],
+                )
+            nc.sync.dma_start(out=out_0[m], in_=x_mid[m][:])
+
+        def inv_rms(m):
+            nc.vector.scalar_tensor_tensor(
+                out=var[m][:], in0=mean_sq[m][:, 0:1], scalar=EPS, in1=mean_sq[m][:, 1:2], op0=ALU.add, op1=ALU.add
+            )
+            nc.gpsimd.tensor_tensor(out=rstd[m][:], in0=var[m][:], in1=minus_half[:], op=ALU.pow)
+
+        def normed(m):
+            nc.vector.scalar_tensor_tensor(
+                out=h_sb[m][:], in0=x_mid[m][:], scalar=rstd[m][:, 0:1], in1=gain_bc[:], op0=ALU.mult, op1=ALU.mult
+            )
+
+        def flip_h(m):
+            flip_and_quantise(h_sb[m][:], h_codes[:, m, :], h_planes[:, m, :])
+
+        def unit(m, c):
+            cols = slice(c * BANK, (c + 1) * BANK)
+            accs = []
+            for w in range(2):
+                acc = psum.tile([P, BANK], F32, tag="bank", name="acc2")
+                for g in range(PASSES):
+                    nc.tensor.matmul_mx(
+                        out=acc[:],
+                        lhsT=h_codes[:, m, g * P : (g + 1) * P].bitcast(FP8X4),
+                        lhsT_scale=h_planes[:, m, g * P : (g + 1) * P],
+                        rhs=w_words[c][w][:, g, :].bitcast(FP8X4),
+                        rhs_scale=w_planes[4 * (PASSES * w + g) : P, cols],
+                        start=(g == 0),
+                        stop=(g == PASSES - 1),
+                    )
+                accs.append(acc)
+            silu = silus.tile([P, BANK], F32, name="silu")
+            nc.scalar.activation(out=silu[:], in_=accs[0][:], func=ACT.Silu)
+            nc.vector.tensor_tensor(out=g_sb[m][:, cols], in0=silu[:], in1=accs[1][:], op=ALU.mult)
+            if c % STORE_CHUNKS == STORE_CHUNKS - 1:
+                done = slice((c + 1 - STORE_CHUNKS) * BANK, (c + 1) * BANK)
+                nc.sync.dma_start(out=out_1[m][:, done], in_=g_sb[m][:, done])
+
+        for m in range(TILES):
+            flip_and_quantise(attn_sb[m][:], a_codes[:, m, :], a_planes[:, m, :])
+        for n in range(2):
+            cols = slice(n * BANK, (n + 1) * BANK)
+            spread = psum.tile([P, BANK], F32, tag="bank", name="spread")
+            nc.tensor.matmul(out=spread[:], lhsT=ones[:], rhs=gain_row[:, cols], start=True, stop=True)
+            nc.scalar.copy(out=gain_bc[:, cols], in_=spread[:])
+        for m in range(TILES):
+            stage1(m)
+        residual(0)
+        residual(1)
+        inv_rms(0)
+        residual(2)
+        normed(0)
+        inv_rms(1)
+        normed(1)
+        flip_h(0)
+        flip_h(1)
+        residual(3)
+        inv_rms(2)
+        inv_rms(3)
+
+        for c in range(CHUNKS):
+            for m in (0, 1):
+                unit(m, c)
+            if c == 0:
+                normed(2)
+                normed(3)
+            if c == 1:
+                flip_h(2)
+                flip_h(3)
+        for c in range(CHUNKS):
+            for m in (2, 3):
+                unit(m, c)

@@ -48,6 +48,13 @@ def tile_transformerblocktpu_pb_kernel(
         nc.vector.memset(minus_half[:], -0.5)
         make_identity(nc, ident[:])
 
+        for q4 in (0, 2, 1, 3):
+            for w, scales in enumerate((w_gate_scales, w_up_scales)):
+                nc.gpsimd.dma_start(
+                    out=w_planes[32 * q4 + 8 * w : 32 * q4 + 8 * w + 8, :].bitcast(F32),
+                    in_=scales[:, 4 * q4 : 4 * q4 + 4, :].bitcast(F32),
+                )
+
         attn_sb = []
         for m in range(TILES):
             t = keep.tile([P, D], BF16, name="attn%d" % m)
@@ -68,12 +75,6 @@ def tile_transformerblocktpu_pb_kernel(
             t = keep.tile([P, D], BF16, name="x%d" % m)
             nc.sync.dma_start(out=t[:], in_=x[m])
             x_sb.append(t)
-        for w, scales in enumerate((w_gate_scales, w_up_scales)):
-            for q4 in range(4):
-                nc.sync.dma_start(
-                    out=w_planes[32 * q4 + 8 * w : 32 * q4 + 8 * w + 8, :].bitcast(I32),
-                    in_=scales[:, 4 * q4 : 4 * q4 + 4, :].bitcast(I32),
-                )
         w_src = [wd.rearrange("g p n t -> p g (n t)").bitcast(I32) for wd in (w_gate_words, w_up_words)]
         w_words = []
         for c in range(CHUNKS):

@@ -16,10 +16,11 @@ P = 128
 TILES = 4
 D = 1024
 M = 4096
-PASSES = D // 512
+K_PASS = 512
+PASSES = D // K_PASS
 BANK = 512
+HALVES = D // BANK
 CHUNKS = M // BANK
-STORE_CHUNKS = 2
 EPS = 1e-6
 
 FLOPS = 2 * TILES * P * D * (D + 2 * M)
@@ -30,128 +31,156 @@ def tile_transformerblocktpu_pb_kernel(
 ):
     nc = tc.nc
     with ExitStack() as ctx:
+        ctx.enter_context(tc.manual_schedule())
         keep = ctx.enter_context(tc.tile_pool(name="keep", bufs=1))
-        stage = ctx.enter_context(tc.tile_pool(name="stage", bufs=2))
-        silus = ctx.enter_context(tc.tile_pool(name="silus", bufs=4))
+        ring = ctx.enter_context(tc.tile_pool(name="ring", bufs=4))
         psum = ctx.enter_context(tc.psum_pool(name="psum", bufs=8))
 
+        minus_half = keep.tile([P, 1], F32)
+        table_warm = keep.tile([P, 1], F32)
         wo_planes = keep.tile([P, D], U8, align_bytes=64)
         w_planes = keep.tile([P, M], U8, align_bytes=64)
         gain_row = keep.tile([P, D], BF16)
         ones = keep.tile([P, P], BF16)
-        minus_half = keep.tile([P, 1], F32)
         ident = keep.tile([P, P], F32)
+        nc.vector.memset(minus_half[:], -0.5)
+        nc.scalar.activation(out=table_warm[:], in_=minus_half[:], func=ACT.Silu)
         nc.vector.memset(wo_planes[:].bitcast(I32), 0)
         nc.vector.memset(gain_row[:], 0.0)
         nc.vector.memset(w_planes[:].bitcast(I32), 0)
         nc.vector.memset(ones[:], 1.0)
-        nc.vector.memset(minus_half[:], -0.5)
         make_identity(nc, ident[:])
 
-        for q4 in (0, 2, 1, 3):
-            for w, scales in enumerate((w_gate_scales, w_up_scales)):
-                nc.gpsimd.dma_start(
-                    out=w_planes[32 * q4 + 8 * w : 32 * q4 + 8 * w + 8, :].bitcast(F32),
-                    in_=scales[:, 4 * q4 : 4 * q4 + 4, :].bitcast(F32),
+        def load_scale_rows(planes, first_plane, scales):
+            for q4 in range(4):
+                top = 32 * q4 + 4 * first_plane
+                nc.sync.dma_start(
+                    out=planes[top : top + 4 * PASSES, :].bitcast(I32),
+                    in_=scales[:, 4 * q4 : 4 * q4 + 4, :].bitcast(I32),
                 )
 
-        attn_sb = []
-        for m in range(TILES):
-            t = keep.tile([P, D], BF16, name="attn%d" % m)
-            nc.sync.dma_start(out=t[:], in_=attn[m])
-            attn_sb.append(t)
-        for q4 in range(4):
-            nc.sync.dma_start(
-                out=wo_planes[32 * q4 : 32 * q4 + 8, :].bitcast(I32),
-                in_=w_o_scales[:, 4 * q4 : 4 * q4 + 4, :].bitcast(I32),
-            )
+        attn_sb = [keep.tile([P, D], BF16, name="attn%d" % m) for m in range(TILES)]
+        x_sb = [keep.tile([P, D], BF16, name="x%d" % m) for m in range(TILES)]
         wo_words = keep.tile([P, PASSES, D], U32, align_bytes=64)
+        w_words = [
+            [keep.tile([P, PASSES, BANK], U32, name="w%d_%d" % (w, c), align_bytes=64) for w in range(2)]
+            for c in range(CHUNKS)
+        ]
+        for m in range(TILES):
+            nc.sync.dma_start(out=attn_sb[m][:], in_=attn[m])
+        load_scale_rows(wo_planes, 0, w_o_scales)
         nc.sync.dma_start(
             out=wo_words[:].bitcast(I32), in_=w_o_words.rearrange("g p n t -> p g (n t)").bitcast(I32)
         )
         nc.sync.dma_start(out=gain_row[0:1, :], in_=rms2_scale.rearrange("(o d) -> o d", o=1))
-        x_sb = []
         for m in range(TILES):
-            t = keep.tile([P, D], BF16, name="x%d" % m)
-            nc.sync.dma_start(out=t[:], in_=x[m])
-            x_sb.append(t)
-        w_src = [wd.rearrange("g p n t -> p g (n t)").bitcast(I32) for wd in (w_gate_words, w_up_words)]
-        w_words = []
+            nc.sync.dma_start(out=x_sb[m][:], in_=x[m])
+        load_scale_rows(w_planes, 0, w_gate_scales)
+        load_scale_rows(w_planes, PASSES, w_up_scales)
         for c in range(CHUNKS):
-            pair = []
-            for w in range(2):
-                t = keep.tile([P, PASSES, BANK], U32, name="w%d_%d" % (w, c), align_bytes=64)
-                nc.sync.dma_start(out=t[:].bitcast(I32), in_=w_src[w][:, :, c * BANK : (c + 1) * BANK])
-                pair.append(t)
-            w_words.append(pair)
+            for w, words in enumerate((w_gate_words, w_up_words)):
+                nc.sync.dma_start(
+                    out=w_words[c][w][:].bitcast(I32),
+                    in_=words.rearrange("g p n t -> p g (n t)").bitcast(I32)[:, :, c * BANK : (c + 1) * BANK],
+                )
 
-        a_codes = keep.tile([P, TILES, PASSES * P], U32, align_bytes=64)
-        a_planes = keep.tile([P, TILES, PASSES * P], U8, align_bytes=64)
-        h_codes = keep.tile([P, TILES, PASSES * P], U32, align_bytes=64)
-        h_planes = keep.tile([P, TILES, PASSES * P], U8, align_bytes=64)
+        a_codes = keep.tile([P, TILES, PASSES, P], U32, align_bytes=64)
+        a_planes = keep.tile([P, TILES, PASSES, P], U8, align_bytes=64)
+        h_codes = keep.tile([P, TILES, PASSES, P], U32, align_bytes=64)
+        h_planes = keep.tile([P, TILES, PASSES, P], U8, align_bytes=64)
         gain_bc = keep.tile([P, D], BF16)
         x_mid = [keep.tile([P, D], F32, name="x_mid%d" % m) for m in range(TILES)]
         g_sb = [keep.tile([P, M], F32, name="g%d" % m) for m in range(TILES)]
-        mean_sq = [keep.tile([P, 2], F32, name="mean_sq%d" % m) for m in range(TILES)]
+        mean_sq = [keep.tile([P, HALVES], F32, name="mean_sq%d" % m) for m in range(TILES)]
         var = [keep.tile([P, 1], F32, name="var%d" % m) for m in range(TILES)]
         rstd = [keep.tile([P, 1], F32, name="rstd%d" % m) for m in range(TILES)]
         h_sb = [keep.tile([P, D], BF16, name="h%d" % m) for m in range(TILES)]
-        s1_banks = {}
+        stage1_acc = {}
+        h_grouped = {}
 
-        def flip_and_quantise(rows, codes, planes):
+        def flip(rows, first_pass, n_passes, tag):
             words = rows.bitcast(F32)
-            flipped = psum.tile([P, PASSES, 2, P], F32, tag="bank", name="flipped")
-            for g in range(PASSES):
+            flipped = psum.tile([P, n_passes, 2, P], F32, tag="bank", name="flipped")
+            for g in range(n_passes):
+                first_word = (K_PASS // 2) * (first_pass + g)
                 for u in range(2):
-                    nc.tensor.transpose(flipped[:, g, u, :], words[:, 256 * g + u : 256 * (g + 1) : 2], ident[:])
-            grouped = stage.tile([P, PASSES * P * 4], BF16, align_bytes=64, name="grouped")
+                    nc.tensor.transpose(
+                        flipped[:, g, u, :], words[:, first_word + u : first_word + K_PASS // 2 : 2], ident[:]
+                    )
+            grouped = ring.tile([P, n_passes * P * 4], BF16, align_bytes=64, tag=tag, name="grouped")
             nc.scalar.copy(
-                out=grouped[:].bitcast(F32).rearrange("p (g r u) -> p g r u", g=PASSES, u=2),
+                out=grouped[:].bitcast(F32).rearrange("p (g r u) -> p g r u", g=n_passes, u=2),
                 in_=flipped[:].rearrange("p g u r -> p g r u"),
             )
+            return grouped
+
+        def quantise(grouped, codes, planes):
             nc.vector.quantize_mx(out=codes.bitcast(FP8X4), scales=planes, in_=grouped[:])
 
+        def quantise_attn(m):
+            grouped = flip(attn_sb[m][:], 0, PASSES, "grouped_attn")
+            quantise(
+                grouped, a_codes[:, m].rearrange("p g r -> p (g r)"), a_planes[:, m].rearrange("p g r -> p (g r)")
+            )
+
+        def spread_gain():
+            for n in range(HALVES):
+                cols = slice(n * BANK, (n + 1) * BANK)
+                spread = psum.tile([P, BANK], F32, tag="bank", name="spread")
+                nc.tensor.matmul(out=spread[:], lhsT=ones[:], rhs=gain_row[:, cols], start=True, stop=True)
+                nc.scalar.copy(out=gain_bc[:, cols], in_=spread[:])
+
         def stage1(m):
-            for n in range(2):
+            for n in range(HALVES):
                 acc = psum.tile([P, BANK], F32, tag="bank", name="acc1")
                 for g in range(PASSES):
                     nc.tensor.matmul_mx(
                         out=acc[:],
-                        lhsT=a_codes[:, m, g * P : (g + 1) * P].bitcast(FP8X4),
-                        lhsT_scale=a_planes[:, m, g * P : (g + 1) * P],
+                        lhsT=a_codes[:, m, g].bitcast(FP8X4),
+                        lhsT_scale=a_planes[:, m, g],
                         rhs=wo_words[:, g, n * BANK : (n + 1) * BANK].bitcast(FP8X4),
                         rhs_scale=wo_planes[4 * g : P, n * BANK : (n + 1) * BANK],
                         start=(g == 0),
                         stop=(g == PASSES - 1),
                     )
-                s1_banks[(m, n)] = acc
+                stage1_acc[(m, n)] = acc
 
         def residual(m):
-            for n in range(2):
+            for n in range(HALVES):
                 cols = slice(n * BANK, (n + 1) * BANK)
-                nc.vector.tensor_tensor(out=x_mid[m][:, cols], in0=s1_banks[(m, n)][:], in1=x_sb[m][:, cols], op=ALU.add)
-                squares = stage.tile([P, BANK], BF16, name="squares")
+                nc.vector.tensor_tensor(
+                    out=x_mid[m][:, cols], in0=stage1_acc[(m, n)][:], in1=x_sb[m][:, cols], op=ALU.add
+                )
+                squares = ring.tile([P, BANK], BF16, name="squares")
                 nc.scalar.activation(
                     out=squares[:], in_=x_mid[m][:, cols], func=ACT.Square, scale=1.0 / 32.0,
                     accum_out=mean_sq[m][:, n : n + 1],
                 )
             nc.sync.dma_start(out=out_0[m], in_=x_mid[m][:])
 
-        def inv_rms(m):
+        def inverse_rms(m):
             nc.vector.scalar_tensor_tensor(
                 out=var[m][:], in0=mean_sq[m][:, 0:1], scalar=EPS, in1=mean_sq[m][:, 1:2], op0=ALU.add, op1=ALU.add
             )
             nc.gpsimd.tensor_tensor(out=rstd[m][:], in0=var[m][:], in1=minus_half[:], op=ALU.pow)
 
         def normed(m):
-            nc.vector.scalar_tensor_tensor(
-                out=h_sb[m][:], in0=x_mid[m][:], scalar=rstd[m][:, 0:1], in1=gain_bc[:], op0=ALU.mult, op1=ALU.mult
-            )
+            for g in range(PASSES):
+                cols = slice(g * K_PASS, (g + 1) * K_PASS)
+                nc.vector.scalar_tensor_tensor(
+                    out=h_sb[m][:, cols], in0=x_mid[m][:, cols], scalar=rstd[m][:, 0:1], in1=gain_bc[:, cols],
+                    op0=ALU.mult, op1=ALU.mult,
+                )
 
         def flip_h(m):
-            flip_and_quantise(h_sb[m][:], h_codes[:, m, :], h_planes[:, m, :])
+            for g in range(PASSES):
+                h_grouped[(m, g)] = flip(h_sb[m][:], g, 1, "grouped_h")
 
-        def unit(m, c):
+        def quantise_h(m):
+            for g in range(PASSES):
+                quantise(h_grouped[(m, g)], h_codes[:, m, g], h_planes[:, m, g])
+
+        def gate_up(m, c):
             cols = slice(c * BANK, (c + 1) * BANK)
             accs = []
             for w in range(2):
@@ -159,52 +188,61 @@ def tile_transformerblocktpu_pb_kernel(
                 for g in range(PASSES):
                     nc.tensor.matmul_mx(
                         out=acc[:],
-                        lhsT=h_codes[:, m, g * P : (g + 1) * P].bitcast(FP8X4),
-                        lhsT_scale=h_planes[:, m, g * P : (g + 1) * P],
+                        lhsT=h_codes[:, m, g].bitcast(FP8X4),
+                        lhsT_scale=h_planes[:, m, g],
                         rhs=w_words[c][w][:, g, :].bitcast(FP8X4),
                         rhs_scale=w_planes[4 * (PASSES * w + g) : P, cols],
                         start=(g == 0),
                         stop=(g == PASSES - 1),
                     )
                 accs.append(acc)
-            silu = silus.tile([P, BANK], F32, name="silu")
+            silu = ring.tile([P, BANK], F32, name="silu")
             nc.scalar.activation(out=silu[:], in_=accs[0][:], func=ACT.Silu)
             nc.vector.tensor_tensor(out=g_sb[m][:, cols], in0=silu[:], in1=accs[1][:], op=ALU.mult)
-            if c % STORE_CHUNKS == STORE_CHUNKS - 1:
-                done = slice((c + 1 - STORE_CHUNKS) * BANK, (c + 1) * BANK)
-                nc.sync.dma_start(out=out_1[m][:, done], in_=g_sb[m][:, done])
+
+        def store_g(m, first_chunk, n_chunks):
+            cols = slice(first_chunk * BANK, (first_chunk + n_chunks) * BANK)
+            nc.sync.dma_start(out=out_1[m][:, cols], in_=g_sb[m][:, cols])
 
         for m in range(TILES):
-            flip_and_quantise(attn_sb[m][:], a_codes[:, m, :], a_planes[:, m, :])
-        for n in range(2):
-            cols = slice(n * BANK, (n + 1) * BANK)
-            spread = psum.tile([P, BANK], F32, tag="bank", name="spread")
-            nc.tensor.matmul(out=spread[:], lhsT=ones[:], rhs=gain_row[:, cols], start=True, stop=True)
-            nc.scalar.copy(out=gain_bc[:, cols], in_=spread[:])
+            quantise_attn(m)
+        spread_gain()
         for m in range(TILES):
             stage1(m)
         residual(0)
         residual(1)
-        inv_rms(0)
+        inverse_rms(0)
         residual(2)
+        inverse_rms(1)
         normed(0)
-        inv_rms(1)
         normed(1)
         flip_h(0)
+        quantise_h(0)
         flip_h(1)
+        quantise_h(1)
         residual(3)
-        inv_rms(2)
-        inv_rms(3)
+        inverse_rms(2)
+        inverse_rms(3)
 
         for c in range(CHUNKS):
             for m in (0, 1):
-                unit(m, c)
+                gate_up(m, c)
+                if c % 2 == 1:
+                    store_g(m, c - 1, 2)
             if c == 0:
                 normed(2)
                 normed(3)
-            if c == 1:
+            if c == 2:
                 flip_h(2)
                 flip_h(3)
+            if c == 3:
+                quantise_h(2)
+                quantise_h(3)
+
         for c in range(CHUNKS):
             for m in (2, 3):
-                unit(m, c)
+                gate_up(m, c)
+                if c >= CHUNKS - 2:
+                    store_g(m, c, 1)
+                elif c % 2 == 1:
+                    store_g(m, c - 1, 2)

@@ -39,7 +39,7 @@ def tile_transformerblocktpu_pb_kernel(
         minus_half = keep.tile([P, 1], F32)
         table_warm = keep.tile([P, 1], F32)
         wo_planes = keep.tile([P, D], U8, align_bytes=64)
-        w_planes = keep.tile([P, M], U8, align_bytes=64)
+        w_planes = keep.tile([P, 2 * PASSES, M // 4], U8, align_bytes=64)
         gain_row = keep.tile([P, D], BF16)
         ones = keep.tile([P, P], BF16)
         ident = keep.tile([P, P], F32)
@@ -47,7 +47,7 @@ def tile_transformerblocktpu_pb_kernel(
         nc.scalar.activation(out=table_warm[:], in_=minus_half[:], func=ACT.Silu)
         nc.vector.memset(wo_planes[:].bitcast(I32), 0)
         nc.vector.memset(gain_row[:], 0.0)
-        nc.vector.memset(w_planes[:].bitcast(I32), 0)
+        nc.vector.memset(w_planes[:].rearrange("p a c -> p (a c)").bitcast(I32), 0)
         nc.vector.memset(ones[:], 1.0)
         make_identity(nc, ident[:])
 
@@ -75,8 +75,13 @@ def tile_transformerblocktpu_pb_kernel(
         nc.sync.dma_start(out=gain_row[0:1, :], in_=rms2_scale.rearrange("(o d) -> o d", o=1))
         for m in range(TILES):
             nc.sync.dma_start(out=x_sb[m][:], in_=x[m])
-        load_scale_rows(w_planes, 0, w_gate_scales)
-        load_scale_rows(w_planes, PASSES, w_up_scales)
+        for w, scales in enumerate((w_gate_scales, w_up_scales)):
+            for g in range(PASSES):
+                for q4 in range(4):
+                    nc.sync.dma_start(
+                        out=w_planes[32 * q4 : 32 * q4 + 16, PASSES * w + g, :].bitcast(I32),
+                        in_=scales[g, 4 * q4 : 4 * q4 + 4, :].bitcast(I32).rearrange("r (s c) -> s r c", s=4),
+                    )
         for c in range(CHUNKS):
             for w, words in enumerate((w_gate_words, w_up_words)):
                 nc.sync.dma_start(
@@ -191,7 +196,7 @@ def tile_transformerblocktpu_pb_kernel(
                         lhsT=h_codes[:, m, g].bitcast(FP8X4),
                         lhsT_scale=h_planes[:, m, g],
                         rhs=w_words[c][w][:, g, :].bitcast(FP8X4),
-                        rhs_scale=w_planes[4 * (PASSES * w + g) : P, cols],
+                        rhs_scale=w_planes[4 * (c // 2) : P, PASSES * w + g, (c % 2) * BANK : (c % 2 + 1) * BANK],
                         start=(g == 0),
                         stop=(g == PASSES - 1),
                     )

@@ -51,14 +51,6 @@ def tile_transformerblocktpu_pb_kernel(
         nc.vector.memset(ones[:], 1.0)
         make_identity(nc, ident[:])
 
-        def load_scale_rows(planes, first_plane, scales):
-            for q4 in range(4):
-                top = 32 * q4 + 4 * first_plane
-                nc.sync.dma_start(
-                    out=planes[top : top + 4 * PASSES, :].bitcast(I32),
-                    in_=scales[:, 4 * q4 : 4 * q4 + 4, :].bitcast(I32),
-                )
-
         attn_sb = [keep.tile([P, D], BF16, name="attn%d" % m) for m in range(TILES)]
         x_sb = [keep.tile([P, D], BF16, name="x%d" % m) for m in range(TILES)]
         wo_words = keep.tile([P, PASSES, D], U32, align_bytes=64)
@@ -66,28 +58,64 @@ def tile_transformerblocktpu_pb_kernel(
             [keep.tile([P, PASSES, BANK], U32, name="w%d_%d" % (w, c), align_bytes=64) for w in range(2)]
             for c in range(CHUNKS)
         ]
-        for m in range(TILES):
+
+        def load_attn(m):
             nc.sync.dma_start(out=attn_sb[m][:], in_=attn[m])
-        load_scale_rows(wo_planes, 0, w_o_scales)
-        nc.sync.dma_start(
-            out=wo_words[:].bitcast(I32), in_=w_o_words.rearrange("g p n t -> p g (n t)").bitcast(I32)
-        )
-        nc.sync.dma_start(out=gain_row[0:1, :], in_=rms2_scale.rearrange("(o d) -> o d", o=1))
-        for m in range(TILES):
+
+        def load_x(m):
             nc.sync.dma_start(out=x_sb[m][:], in_=x[m])
-        for w, scales in enumerate((w_gate_scales, w_up_scales)):
-            for g in range(PASSES):
-                for q4 in range(4):
-                    nc.sync.dma_start(
-                        out=w_planes[32 * q4 : 32 * q4 + 16, PASSES * w + g, :].bitcast(I32),
-                        in_=scales[g, 4 * q4 : 4 * q4 + 4, :].bitcast(I32).rearrange("r (s c) -> s r c", s=4),
-                    )
-        for c in range(CHUNKS):
+
+        def load_gain():
+            nc.sync.dma_start(out=gain_row[0:1, :], in_=rms2_scale.rearrange("(o d) -> o d", o=1))
+
+        def load_wo_scales():
+            for q4 in range(4):
+                nc.sync.dma_start(
+                    out=wo_planes[32 * q4 : 32 * q4 + 4 * PASSES, :].bitcast(I32),
+                    in_=w_o_scales[:, 4 * q4 : 4 * q4 + 4, :].bitcast(I32),
+                )
+
+        def load_wo():
+            nc.sync.dma_start(
+                out=wo_words[:].bitcast(I32), in_=w_o_words.rearrange("g p n t -> p g (n t)").bitcast(I32)
+            )
+
+        def load_w_scales(first, count):
+            for i in range(first, first + count):
+                area, q4 = divmod(i, 4)
+                scales = (w_gate_scales, w_up_scales)[area // PASSES]
+                nc.sync.dma_start(
+                    out=w_planes[32 * q4 : 32 * q4 + 16, area, :].bitcast(I32),
+                    in_=scales[area % PASSES, 4 * q4 : 4 * q4 + 4, :].bitcast(I32).rearrange("r (s c) -> s r c", s=4),
+                )
+
+        def load_w(c):
             for w, words in enumerate((w_gate_words, w_up_words)):
                 nc.sync.dma_start(
                     out=w_words[c][w][:].bitcast(I32),
                     in_=words.rearrange("g p n t -> p g (n t)").bitcast(I32)[:, :, c * BANK : (c + 1) * BANK],
                 )
+
+        load_attn(0)
+        load_attn(1)
+        load_attn(2)
+        load_attn(3)
+        load_wo_scales()
+        load_wo()
+        load_gain()
+        load_x(0)
+        load_x(1)
+        load_x(2)
+        load_x(3)
+        load_w_scales(0, 16)
+        load_w(0)
+        load_w(1)
+        load_w(2)
+        load_w(3)
+        load_w(4)
+        load_w(5)
+        load_w(6)
+        load_w(7)
 
         a_codes = keep.tile([P, TILES, PASSES, P], U32, align_bytes=64)
         a_planes = keep.tile([P, TILES, PASSES, P], U8, align_bytes=64)
@@ -100,67 +128,86 @@ def tile_transformerblocktpu_pb_kernel(
         var = [keep.tile([P, 1], F32, name="var%d" % m) for m in range(TILES)]
         rstd = [keep.tile([P, 1], F32, name="rstd%d" % m) for m in range(TILES)]
         h_sb = [keep.tile([P, D], BF16, name="h%d" % m) for m in range(TILES)]
+        flipped = {}
+        grouped = {}
+        spread = {}
         stage1_acc = {}
-        h_grouped = {}
+        stage2_acc = {}
+        silu_sb = {}
 
-        def flip(rows, first_pass, n_passes, tag):
+        def flip(key, rows, first_pass, n_passes, banks):
             words = rows.bitcast(F32)
-            flipped = psum.tile([P, n_passes, 2, P], F32, tag="bank", name="flipped")
+            turned = psum.tile([P, n_passes, 2, P], F32, tag=banks, name="turned")
             for g in range(n_passes):
                 first_word = (K_PASS // 2) * (first_pass + g)
                 for u in range(2):
                     nc.tensor.transpose(
-                        flipped[:, g, u, :], words[:, first_word + u : first_word + K_PASS // 2 : 2], ident[:]
+                        turned[:, g, u, :], words[:, first_word + u : first_word + K_PASS // 2 : 2], ident[:]
                     )
-            grouped = ring.tile([P, n_passes * P * 4], BF16, align_bytes=64, tag=tag, name="grouped")
-            nc.scalar.copy(
-                out=grouped[:].bitcast(F32).rearrange("p (g r u) -> p g r u", g=n_passes, u=2),
-                in_=flipped[:].rearrange("p g u r -> p g r u"),
-            )
-            return grouped
+            flipped[key] = turned
 
-        def quantise(grouped, codes, planes):
-            nc.vector.quantize_mx(out=codes.bitcast(FP8X4), scales=planes, in_=grouped[:])
+        def group(key, n_passes, tag):
+            tile = ring.tile([P, n_passes * P * 4], BF16, align_bytes=64, tag=tag, name="tile")
+            nc.scalar.copy(
+                out=tile[:].bitcast(F32).rearrange("p (g r u) -> p g r u", g=n_passes, u=2),
+                in_=flipped[key][:].rearrange("p g u r -> p g r u"),
+            )
+            grouped[key] = tile
+
+        def flip_attn(m, banks):
+            flip(("a", m), attn_sb[m][:], 0, PASSES, banks)
+
+        def group_attn(m):
+            group(("a", m), PASSES, "grouped_attn")
 
         def quantise_attn(m):
-            grouped = flip(attn_sb[m][:], 0, PASSES, "grouped_attn")
-            quantise(
-                grouped, a_codes[:, m].rearrange("p g r -> p (g r)"), a_planes[:, m].rearrange("p g r -> p (g r)")
+            nc.vector.quantize_mx(
+                out=a_codes[:, m].rearrange("p g r -> p (g r)").bitcast(FP8X4),
+                scales=a_planes[:, m].rearrange("p g r -> p (g r)"),
+                in_=grouped[("a", m)][:],
             )
 
-        def spread_gain():
-            for n in range(HALVES):
-                cols = slice(n * BANK, (n + 1) * BANK)
-                spread = psum.tile([P, BANK], F32, tag="bank", name="spread")
-                nc.tensor.matmul(out=spread[:], lhsT=ones[:], rhs=gain_row[:, cols], start=True, stop=True)
-                nc.scalar.copy(out=gain_bc[:, cols], in_=spread[:])
+        def spread_gain(n, banks):
+            acc = psum.tile([P, BANK], F32, tag=banks, name="acc0")
+            nc.tensor.matmul(out=acc[:], lhsT=ones[:], rhs=gain_row[:, n * BANK : (n + 1) * BANK], start=True, stop=True)
+            spread[n] = acc
 
-        def stage1(m):
-            for n in range(HALVES):
-                acc = psum.tile([P, BANK], F32, tag="bank", name="acc1")
-                for g in range(PASSES):
-                    nc.tensor.matmul_mx(
-                        out=acc[:],
-                        lhsT=a_codes[:, m, g].bitcast(FP8X4),
-                        lhsT_scale=a_planes[:, m, g],
-                        rhs=wo_words[:, g, n * BANK : (n + 1) * BANK].bitcast(FP8X4),
-                        rhs_scale=wo_planes[4 * g : P, n * BANK : (n + 1) * BANK],
-                        start=(g == 0),
-                        stop=(g == PASSES - 1),
-                    )
-                stage1_acc[(m, n)] = acc
+        def keep_gain(n):
+            nc.scalar.copy(out=gain_bc[:, n * BANK : (n + 1) * BANK], in_=spread[n][:])
 
-        def residual(m):
-            for n in range(HALVES):
-                cols = slice(n * BANK, (n + 1) * BANK)
-                nc.vector.tensor_tensor(
-                    out=x_mid[m][:, cols], in0=stage1_acc[(m, n)][:], in1=x_sb[m][:, cols], op=ALU.add
+        def keep_warm(banks):
+            idle = psum.tile([P, BANK], F32, tag=banks, name="idle")
+            for i in range(2):
+                nc.tensor.matmul(out=idle[:], lhsT=ones[:], rhs=gain_row[:, 0:BANK], start=True, stop=True)
+
+        def stage1(m, n, banks):
+            acc = psum.tile([P, BANK], F32, tag=banks, name="acc1")
+            for g in range(PASSES):
+                nc.tensor.matmul_mx(
+                    out=acc[:],
+                    lhsT=a_codes[:, m, g].bitcast(FP8X4),
+                    lhsT_scale=a_planes[:, m, g],
+                    rhs=wo_words[:, g, n * BANK : (n + 1) * BANK].bitcast(FP8X4),
+                    rhs_scale=wo_planes[4 * g : P, n * BANK : (n + 1) * BANK],
+                    start=(g == 0),
+                    stop=(g == PASSES - 1),
                 )
-                squares = ring.tile([P, BANK], BF16, name="squares")
-                nc.scalar.activation(
-                    out=squares[:], in_=x_mid[m][:, cols], func=ACT.Square, scale=1.0 / 32.0,
-                    accum_out=mean_sq[m][:, n : n + 1],
-                )
+            stage1_acc[(m, n)] = acc
+
+        def residual(m, n):
+            cols = slice(n * BANK, (n + 1) * BANK)
+            nc.vector.tensor_tensor(
+                out=x_mid[m][:, cols], in0=stage1_acc[(m, n)][:], in1=x_sb[m][:, cols], op=ALU.add
+            )
+
+        def squares(m, n):
+            junk = ring.tile([P, BANK], BF16, name="junk")
+            nc.scalar.activation(
+                out=junk[:], in_=x_mid[m][:, n * BANK : (n + 1) * BANK], func=ACT.Square, scale=1.0 / 32.0,
+                accum_out=mean_sq[m][:, n : n + 1],
+            )
+
+        def store_x_mid(m):
             nc.sync.dma_start(out=out_0[m], in_=x_mid[m][:])
 
         def inverse_rms(m):
@@ -169,85 +216,257 @@ def tile_transformerblocktpu_pb_kernel(
             )
             nc.gpsimd.tensor_tensor(out=rstd[m][:], in0=var[m][:], in1=minus_half[:], op=ALU.pow)
 
-        def normed(m):
-            for g in range(PASSES):
-                cols = slice(g * K_PASS, (g + 1) * K_PASS)
-                nc.vector.scalar_tensor_tensor(
-                    out=h_sb[m][:, cols], in0=x_mid[m][:, cols], scalar=rstd[m][:, 0:1], in1=gain_bc[:, cols],
-                    op0=ALU.mult, op1=ALU.mult,
-                )
+        def normed(m, g):
+            cols = slice(g * K_PASS, (g + 1) * K_PASS)
+            nc.vector.scalar_tensor_tensor(
+                out=h_sb[m][:, cols], in0=x_mid[m][:, cols], scalar=rstd[m][:, 0:1], in1=gain_bc[:, cols],
+                op0=ALU.mult, op1=ALU.mult,
+            )
 
-        def flip_h(m):
-            for g in range(PASSES):
-                h_grouped[(m, g)] = flip(h_sb[m][:], g, 1, "grouped_h")
+        def flip_h(m, g, banks):
+            flip(("h", m, g), h_sb[m][:], g, 1, banks)
 
-        def quantise_h(m):
-            for g in range(PASSES):
-                quantise(h_grouped[(m, g)], h_codes[:, m, g], h_planes[:, m, g])
+        def group_h(m, g):
+            group(("h", m, g), 1, "grouped_h")
 
-        def gate_up(m, c):
-            cols = slice(c * BANK, (c + 1) * BANK)
+        def quantise_h(m, g):
+            nc.vector.quantize_mx(
+                out=h_codes[:, m, g].bitcast(FP8X4), scales=h_planes[:, m, g], in_=grouped[("h", m, g)][:]
+            )
+
+        def gate_up(m, c, banks, first=0, width=BANK):
             accs = []
             for w in range(2):
-                acc = psum.tile([P, BANK], F32, tag="bank", name="acc2")
+                acc = psum.tile([P, width], F32, tag=banks, name="acc2")
                 for g in range(PASSES):
                     nc.tensor.matmul_mx(
                         out=acc[:],
                         lhsT=h_codes[:, m, g].bitcast(FP8X4),
                         lhsT_scale=h_planes[:, m, g],
-                        rhs=w_words[c][w][:, g, :].bitcast(FP8X4),
-                        rhs_scale=w_planes[4 * (c // 2) : P, PASSES * w + g, (c % 2) * BANK : (c % 2 + 1) * BANK],
+                        rhs=w_words[c][w][:, g, first : first + width].bitcast(FP8X4),
+                        rhs_scale=w_planes[
+                            4 * (c // 2) : P, PASSES * w + g, (c % 2) * BANK + first : (c % 2) * BANK + first + width
+                        ],
                         start=(g == 0),
                         stop=(g == PASSES - 1),
                     )
                 accs.append(acc)
-            silu = ring.tile([P, BANK], F32, name="silu")
-            nc.scalar.activation(out=silu[:], in_=accs[0][:], func=ACT.Silu)
-            nc.vector.tensor_tensor(out=g_sb[m][:, cols], in0=silu[:], in1=accs[1][:], op=ALU.mult)
+            stage2_acc[(m, c, first)] = accs
+
+        def silu(m, c, first=0, width=BANK):
+            tile = ring.tile([P, width], F32, name="silu_tile")
+            nc.scalar.activation(out=tile[:], in_=stage2_acc[(m, c, first)][0][:], func=ACT.Silu)
+            silu_sb[(m, c, first)] = tile
+
+        def product(m, c, first=0, width=BANK):
+            nc.vector.tensor_tensor(
+                out=g_sb[m][:, c * BANK + first : c * BANK + first + width], in0=silu_sb[(m, c, first)][:],
+                in1=stage2_acc[(m, c, first)][1][:], op=ALU.mult,
+            )
+
+        def store_part(m, c, first, width):
+            cols = slice(c * BANK + first, c * BANK + first + width)
+            nc.sync.dma_start(out=out_1[m][:, cols], in_=g_sb[m][:, cols])
 
         def store_g(m, first_chunk, n_chunks):
             cols = slice(first_chunk * BANK, (first_chunk + n_chunks) * BANK)
             nc.sync.dma_start(out=out_1[m][:, cols], in_=g_sb[m][:, cols])
 
-        for m in range(TILES):
-            quantise_attn(m)
-        spread_gain()
-        for m in range(TILES):
-            stage1(m)
-        residual(0)
-        residual(1)
+        flip_attn(0, "bank")
+        group_attn(0)
+        quantise_attn(0)
+        flip_attn(1, "bank")
+        group_attn(1)
+        quantise_attn(1)
+        flip_attn(2, "bank")
+        group_attn(2)
+        quantise_attn(2)
+        flip_attn(3, "bank")
+        group_attn(3)
+        quantise_attn(3)
+        spread_gain(0, "bank")
+        keep_gain(0)
+        spread_gain(1, "bank")
+        keep_gain(1)
+        stage1(0, 0, "bank")
+        stage1(0, 1, "bank")
+        stage1(1, 0, "bank")
+        stage1(1, 1, "bank")
+        stage1(2, 0, "bank")
+        stage1(2, 1, "bank")
+        stage1(3, 0, "bank")
+        stage1(3, 1, "bank")
+        residual(0, 0)
+        squares(0, 0)
+        residual(0, 1)
+        squares(0, 1)
+        store_x_mid(0)
+        residual(1, 0)
+        squares(1, 0)
+        residual(1, 1)
+        squares(1, 1)
+        store_x_mid(1)
         inverse_rms(0)
-        residual(2)
+        residual(2, 0)
+        squares(2, 0)
+        residual(2, 1)
+        squares(2, 1)
+        store_x_mid(2)
         inverse_rms(1)
-        normed(0)
-        normed(1)
-        flip_h(0)
-        quantise_h(0)
-        flip_h(1)
-        quantise_h(1)
-        residual(3)
+        normed(0, 0)
+        normed(0, 1)
+        normed(1, 0)
+        normed(1, 1)
+        flip_h(0, 0, "bank")
+        group_h(0, 0)
+        flip_h(0, 1, "bank")
+        group_h(0, 1)
+        quantise_h(0, 0)
+        quantise_h(0, 1)
+        flip_h(1, 0, "bank")
+        group_h(1, 0)
+        flip_h(1, 1, "bank")
+        group_h(1, 1)
+        quantise_h(1, 0)
+        quantise_h(1, 1)
+        residual(3, 0)
+        squares(3, 0)
+        residual(3, 1)
+        squares(3, 1)
+        store_x_mid(3)
         inverse_rms(2)
         inverse_rms(3)
-
-        for c in range(CHUNKS):
-            for m in (0, 1):
-                gate_up(m, c)
-                if c % 2 == 1:
-                    store_g(m, c - 1, 2)
-            if c == 0:
-                normed(2)
-                normed(3)
-            if c == 2:
-                flip_h(2)
-                flip_h(3)
-            if c == 3:
-                quantise_h(2)
-                quantise_h(3)
-
-        for c in range(CHUNKS):
-            for m in (2, 3):
-                gate_up(m, c)
-                if c >= CHUNKS - 2:
-                    store_g(m, c, 1)
-                elif c % 2 == 1:
-                    store_g(m, c - 1, 2)
+        gate_up(0, 0, "bank")
+        silu(0, 0)
+        product(0, 0)
+        gate_up(1, 0, "bank")
+        silu(1, 0)
+        product(1, 0)
+        normed(2, 0)
+        normed(2, 1)
+        normed(3, 0)
+        normed(3, 1)
+        gate_up(0, 1, "bank")
+        silu(0, 1)
+        product(0, 1)
+        store_g(0, 0, 2)
+        gate_up(1, 1, "bank")
+        silu(1, 1)
+        product(1, 1)
+        store_g(1, 0, 2)
+        gate_up(0, 2, "bank")
+        silu(0, 2)
+        product(0, 2)
+        gate_up(1, 2, "bank")
+        silu(1, 2)
+        product(1, 2)
+        flip_h(2, 0, "bank")
+        group_h(2, 0)
+        flip_h(2, 1, "bank")
+        group_h(2, 1)
+        flip_h(3, 0, "bank")
+        group_h(3, 0)
+        flip_h(3, 1, "bank")
+        group_h(3, 1)
+        gate_up(0, 3, "bank")
+        silu(0, 3)
+        product(0, 3)
+        store_g(0, 2, 2)
+        gate_up(1, 3, "bank")
+        silu(1, 3)
+        product(1, 3)
+        store_g(1, 2, 2)
+        quantise_h(2, 0)
+        quantise_h(2, 1)
+        quantise_h(3, 0)
+        quantise_h(3, 1)
+        gate_up(0, 4, "bank")
+        silu(0, 4)
+        product(0, 4)
+        gate_up(1, 4, "bank")
+        silu(1, 4)
+        product(1, 4)
+        gate_up(0, 5, "bank")
+        silu(0, 5)
+        product(0, 5)
+        store_g(0, 4, 2)
+        gate_up(1, 5, "bank")
+        silu(1, 5)
+        product(1, 5)
+        store_g(1, 4, 2)
+        gate_up(0, 6, "bank")
+        silu(0, 6)
+        product(0, 6)
+        gate_up(1, 6, "bank")
+        silu(1, 6)
+        product(1, 6)
+        gate_up(0, 7, "bank")
+        silu(0, 7)
+        product(0, 7)
+        store_g(0, 6, 2)
+        gate_up(1, 7, "bank")
+        silu(1, 7)
+        product(1, 7)
+        store_g(1, 6, 2)
+        gate_up(2, 0, "bank")
+        silu(2, 0)
+        product(2, 0)
+        gate_up(3, 0, "bank")
+        silu(3, 0)
+        product(3, 0)
+        gate_up(2, 1, "bank")
+        silu(2, 1)
+        product(2, 1)
+        store_g(2, 0, 2)
+        gate_up(3, 1, "bank")
+        silu(3, 1)
+        product(3, 1)
+        store_g(3, 0, 2)
+        gate_up(2, 2, "bank")
+        silu(2, 2)
+        product(2, 2)
+        gate_up(3, 2, "bank")
+        silu(3, 2)
+        product(3, 2)
+        gate_up(2, 3, "bank")
+        silu(2, 3)
+        product(2, 3)
+        store_g(2, 2, 2)
+        gate_up(3, 3, "bank")
+        silu(3, 3)
+        product(3, 3)
+        store_g(3, 2, 2)
+        gate_up(2, 4, "bank")
+        silu(2, 4)
+        product(2, 4)
+        gate_up(3, 4, "bank")
+        silu(3, 4)
+        product(3, 4)
+        gate_up(2, 5, "bank")
+        silu(2, 5)
+        product(2, 5)
+        store_g(2, 4, 2)
+        gate_up(3, 5, "bank")
+        silu(3, 5)
+        product(3, 5)
+        store_g(3, 4, 2)
+        gate_up(2, 6, "bank")
+        silu(2, 6)
+        product(2, 6)
+        store_g(2, 6, 1)
+        gate_up(3, 6, "bank")
+        silu(3, 6)
+        product(3, 6)
+        store_g(3, 6, 1)
+        gate_up(2, 7, "bank")
+        silu(2, 7)
+        product(2, 7)
+        store_g(2, 7, 1)
+        gate_up(3, 7, "bank", 0, BANK // 2)
+        silu(3, 7, 0, BANK // 2)
+        gate_up(3, 7, "bank", BANK // 2, BANK // 2)
+        product(3, 7, 0, BANK // 2)
+        store_part(3, 7, 0, BANK // 2)
+        silu(3, 7, BANK // 2, BANK // 2)
+        product(3, 7, BANK // 2, BANK // 2)
+        store_part(3, 7, BANK // 2, BANK // 2)

@@ -21,6 +21,7 @@ PASSES = D // K_PASS
 BANK = 512
 HALVES = D // BANK
 CHUNKS = M // BANK
+LOADS = (1, 1, 1, 1, 1, 1, 1, 1)
 EPS = 1e-6
 
 FLOPS = 2 * TILES * P * D * (D + 2 * M)
@@ -45,8 +46,8 @@ def tile_transformerblocktpu_pb_kernel(
         ident = keep.tile([P, P], F32)
         nc.vector.memset(minus_half[:], -0.5)
         nc.scalar.activation(out=table_warm[:], in_=minus_half[:], func=ACT.Silu)
+        nc.vector.memset(gain_row[:].bitcast(I32), 0)
         nc.vector.memset(wo_planes[:].bitcast(I32), 0)
-        nc.vector.memset(gain_row[:], 0.0)
         nc.vector.memset(w_planes[:].rearrange("p a c -> p (a c)").bitcast(I32), 0)
         nc.vector.memset(ones[:], 1.0)
         make_identity(nc, ident[:])
@@ -54,10 +55,11 @@ def tile_transformerblocktpu_pb_kernel(
         attn_sb = [keep.tile([P, D], BF16, name="attn%d" % m) for m in range(TILES)]
         x_sb = [keep.tile([P, D], BF16, name="x%d" % m) for m in range(TILES)]
         wo_words = keep.tile([P, PASSES, D], U32, align_bytes=64)
-        w_words = [
-            [keep.tile([P, PASSES, BANK], U32, name="w%d_%d" % (w, c), align_bytes=64) for w in range(2)]
-            for c in range(CHUNKS)
+        w_pieces = [
+            [keep.tile([P, PASSES, n * BANK], U32, name="w%d_%d" % (w, i), align_bytes=64) for w in range(2)]
+            for i, n in enumerate(LOADS)
         ]
+        where = [(i, j) for i, n in enumerate(LOADS) for j in range(n)]
 
         def load_attn(m):
             nc.sync.dma_start(out=attn_sb[m][:], in_=attn[m])
@@ -89,20 +91,21 @@ def tile_transformerblocktpu_pb_kernel(
                     in_=scales[area % PASSES, 4 * q4 : 4 * q4 + 4, :].bitcast(I32).rearrange("r (s c) -> s r c", s=4),
                 )
 
-        def load_w(c):
+        def load_w(i):
+            first = sum(LOADS[:i]) * BANK
             for w, words in enumerate((w_gate_words, w_up_words)):
                 nc.sync.dma_start(
-                    out=w_words[c][w][:].bitcast(I32),
-                    in_=words.rearrange("g p n t -> p g (n t)").bitcast(I32)[:, :, c * BANK : (c + 1) * BANK],
+                    out=w_pieces[i][w][:].bitcast(I32),
+                    in_=words.rearrange("g p n t -> p g (n t)").bitcast(I32)[:, :, first : first + LOADS[i] * BANK],
                 )
 
         load_attn(0)
         load_attn(1)
+        load_gain()
         load_attn(2)
         load_attn(3)
-        load_wo_scales()
         load_wo()
-        load_gain()
+        load_wo_scales()
         load_x(0)
         load_x(1)
         load_x(2)
@@ -243,7 +246,9 @@ def tile_transformerblocktpu_pb_kernel(
                         out=acc[:],
                         lhsT=h_codes[:, m, g].bitcast(FP8X4),
                         lhsT_scale=h_planes[:, m, g],
-                        rhs=w_words[c][w][:, g, first : first + width].bitcast(FP8X4),
+                        rhs=w_pieces[where[c][0]][w][
+                            :, g, where[c][1] * BANK + first : where[c][1] * BANK + first + width
+                        ].bitcast(FP8X4),
                         rhs_scale=w_planes[
                             4 * (c // 2) : P, PASSES * w + g, (c % 2) * BANK + first : (c % 2) * BANK + first + width
                         ],

@@ -82,6 +82,13 @@ def tile_transformerblocktpu_pb_kernel(
                 out=wo_words[:].bitcast(I32), in_=w_o_words.rearrange("g p n t -> p g (n t)").bitcast(I32)
             )
 
+        def load_wo_half(n):
+            cols = slice(n * BANK, (n + 1) * BANK)
+            nc.sync.dma_start(
+                out=wo_words[:, :, cols].bitcast(I32),
+                in_=w_o_words.rearrange("g p n t -> p g (n t)").bitcast(I32)[:, :, cols],
+            )
+
         def load_w_scales(first, count):
             for i in range(first, first + count):
                 area, q4 = divmod(i, 4)
@@ -104,8 +111,9 @@ def tile_transformerblocktpu_pb_kernel(
         load_gain()
         load_attn(2)
         load_attn(3)
-        load_wo()
+        load_wo_half(0)
         load_wo_scales()
+        load_wo_half(1)
         load_x(0)
         load_x(1)
         load_x(2)
@@ -178,10 +186,9 @@ def tile_transformerblocktpu_pb_kernel(
         def keep_gain(n):
             nc.scalar.copy(out=gain_bc[:, n * BANK : (n + 1) * BANK], in_=spread[n][:])
 
-        def keep_warm(banks):
-            idle = psum.tile([P, BANK], F32, tag=banks, name="idle")
+        def keep_warm(spent):
             for i in range(2):
-                nc.tensor.matmul(out=idle[:], lhsT=ones[:], rhs=gain_row[:, 0:BANK], start=True, stop=True)
+                nc.tensor.matmul(out=spent, lhsT=ones[:], rhs=gain_row[:, 0:BANK], start=True, stop=True)
 
         def stage1(m, n, banks):
             acc = psum.tile([P, BANK], F32, tag=banks, name="acc1")

@@ -35,7 +35,7 @@ def tile_transformerblocktpu_pb_kernel(
         ctx.enter_context(tc.manual_schedule())
         keep = ctx.enter_context(tc.tile_pool(name="keep", bufs=1))
         ring = ctx.enter_context(tc.tile_pool(name="ring", bufs=4))
-        psum = ctx.enter_context(tc.psum_pool(name="psum", bufs=8))
+        psum = ctx.enter_context(tc.psum_pool(name="psum", bufs=4))
 
         minus_half = keep.tile([P, 1], F32)
         table_warm = keep.tile([P, 1], F32)
@@ -116,10 +116,13 @@ def tile_transformerblocktpu_pb_kernel(
         load_wo_half(1)
         load_x(0)
         load_x(1)
+        load_w_scales(0, 4)
         load_x(2)
+        load_w_scales(4, 4)
         load_x(3)
-        load_w_scales(0, 16)
+        load_w_scales(8, 4)
         load_w(0)
+        load_w_scales(12, 4)
         load_w(1)
         load_w(2)
         load_w(3)
@@ -284,30 +287,30 @@ def tile_transformerblocktpu_pb_kernel(
             cols = slice(first_chunk * BANK, (first_chunk + n_chunks) * BANK)
             nc.sync.dma_start(out=out_1[m][:, cols], in_=g_sb[m][:, cols])
 
-        flip_attn(0, "bank")
+        flip_attn(0, "lo")
         group_attn(0)
         quantise_attn(0)
-        flip_attn(1, "bank")
+        flip_attn(1, "lo")
         group_attn(1)
         quantise_attn(1)
-        flip_attn(2, "bank")
+        flip_attn(2, "lo")
         group_attn(2)
         quantise_attn(2)
-        flip_attn(3, "bank")
+        flip_attn(3, "lo")
         group_attn(3)
         quantise_attn(3)
-        spread_gain(0, "bank")
+        spread_gain(0, "hi")
         keep_gain(0)
-        spread_gain(1, "bank")
+        spread_gain(1, "hi")
         keep_gain(1)
-        stage1(0, 0, "bank")
-        stage1(0, 1, "bank")
-        stage1(1, 0, "bank")
-        stage1(1, 1, "bank")
-        stage1(2, 0, "bank")
-        stage1(2, 1, "bank")
-        stage1(3, 0, "bank")
-        stage1(3, 1, "bank")
+        stage1(0, 0, "lo")
+        stage1(0, 1, "lo")
+        stage1(1, 0, "lo")
+        stage1(1, 1, "lo")
+        stage1(2, 0, "hi")
+        stage1(2, 1, "hi")
+        stage1(3, 0, "hi")
+        stage1(3, 1, "hi")
         residual(0, 0)
         squares(0, 0)
         residual(0, 1)
@@ -329,154 +332,154 @@ def tile_transformerblocktpu_pb_kernel(
         normed(0, 1)
         normed(1, 0)
         normed(1, 1)
-        flip_h(0, 0, "bank")
+        flip_h(0, 0, "lo")
         group_h(0, 0)
-        flip_h(0, 1, "bank")
+        flip_h(0, 1, "lo")
         group_h(0, 1)
         quantise_h(0, 0)
         quantise_h(0, 1)
-        flip_h(1, 0, "bank")
+        flip_h(1, 0, "lo")
         group_h(1, 0)
-        flip_h(1, 1, "bank")
+        flip_h(1, 1, "lo")
         group_h(1, 1)
         quantise_h(1, 0)
         quantise_h(1, 1)
+        gate_up(0, 0, "lo")
+        silu(0, 0)
+        gate_up(1, 0, "lo")
+        silu(1, 0)
         residual(3, 0)
         squares(3, 0)
         residual(3, 1)
         squares(3, 1)
         store_x_mid(3)
         inverse_rms(2)
-        inverse_rms(3)
-        gate_up(0, 0, "bank")
-        silu(0, 0)
         product(0, 0)
-        gate_up(1, 0, "bank")
-        silu(1, 0)
+        inverse_rms(3)
         product(1, 0)
+        gate_up(0, 1, "hi")
+        silu(0, 1)
+        product(0, 1)
+        store_g(0, 0, 2)
+        gate_up(1, 1, "hi")
+        silu(1, 1)
+        product(1, 1)
+        store_g(1, 0, 2)
+        gate_up(0, 2, "lo")
+        silu(0, 2)
+        product(0, 2)
+        gate_up(1, 2, "lo")
+        silu(1, 2)
+        product(1, 2)
         normed(2, 0)
         normed(2, 1)
         normed(3, 0)
         normed(3, 1)
-        gate_up(0, 1, "bank")
-        silu(0, 1)
-        product(0, 1)
-        store_g(0, 0, 2)
-        gate_up(1, 1, "bank")
-        silu(1, 1)
-        product(1, 1)
-        store_g(1, 0, 2)
-        gate_up(0, 2, "bank")
-        silu(0, 2)
-        product(0, 2)
-        gate_up(1, 2, "bank")
-        silu(1, 2)
-        product(1, 2)
-        flip_h(2, 0, "bank")
-        group_h(2, 0)
-        flip_h(2, 1, "bank")
-        group_h(2, 1)
-        flip_h(3, 0, "bank")
-        group_h(3, 0)
-        flip_h(3, 1, "bank")
-        group_h(3, 1)
-        gate_up(0, 3, "bank")
+        gate_up(0, 3, "hi")
         silu(0, 3)
         product(0, 3)
         store_g(0, 2, 2)
-        gate_up(1, 3, "bank")
+        gate_up(1, 3, "hi")
         silu(1, 3)
         product(1, 3)
         store_g(1, 2, 2)
+        gate_up(0, 4, "lo")
+        silu(0, 4)
+        product(0, 4)
+        gate_up(1, 4, "lo")
+        silu(1, 4)
+        product(1, 4)
+        flip_h(2, 0, "hi")
+        group_h(2, 0)
+        flip_h(2, 1, "hi")
+        group_h(2, 1)
+        flip_h(3, 0, "hi")
+        group_h(3, 0)
+        flip_h(3, 1, "hi")
+        group_h(3, 1)
+        gate_up(0, 5, "lo")
+        silu(0, 5)
+        product(0, 5)
+        store_g(0, 4, 2)
+        gate_up(1, 5, "lo")
+        silu(1, 5)
+        product(1, 5)
+        store_g(1, 4, 2)
         quantise_h(2, 0)
         quantise_h(2, 1)
         quantise_h(3, 0)
         quantise_h(3, 1)
-        gate_up(0, 4, "bank")
-        silu(0, 4)
-        product(0, 4)
-        gate_up(1, 4, "bank")
-        silu(1, 4)
-        product(1, 4)
-        gate_up(0, 5, "bank")
-        silu(0, 5)
-        product(0, 5)
-        store_g(0, 4, 2)
-        gate_up(1, 5, "bank")
-        silu(1, 5)
-        product(1, 5)
-        store_g(1, 4, 2)
-        gate_up(0, 6, "bank")
+        gate_up(0, 6, "hi")
         silu(0, 6)
         product(0, 6)
-        gate_up(1, 6, "bank")
+        gate_up(1, 6, "hi")
         silu(1, 6)
         product(1, 6)
-        gate_up(0, 7, "bank")
+        gate_up(0, 7, "lo")
         silu(0, 7)
         product(0, 7)
         store_g(0, 6, 2)
-        gate_up(1, 7, "bank")
+        gate_up(1, 7, "lo")
         silu(1, 7)
         product(1, 7)
         store_g(1, 6, 2)
-        gate_up(2, 0, "bank")
+        gate_up(2, 0, "hi")
         silu(2, 0)
         product(2, 0)
-        gate_up(3, 0, "bank")
+        gate_up(3, 0, "hi")
         silu(3, 0)
         product(3, 0)
-        gate_up(2, 1, "bank")
+        gate_up(2, 1, "lo")
         silu(2, 1)
         product(2, 1)
         store_g(2, 0, 2)
-        gate_up(3, 1, "bank")
+        gate_up(3, 1, "lo")
         silu(3, 1)
         product(3, 1)
         store_g(3, 0, 2)
-        gate_up(2, 2, "bank")
+        gate_up(2, 2, "hi")
         silu(2, 2)
         product(2, 2)
-        gate_up(3, 2, "bank")
+        gate_up(3, 2, "hi")
         silu(3, 2)
         product(3, 2)
-        gate_up(2, 3, "bank")
+        gate_up(2, 3, "lo")
         silu(2, 3)
         product(2, 3)
         store_g(2, 2, 2)
-        gate_up(3, 3, "bank")
+        gate_up(3, 3, "lo")
         silu(3, 3)
         product(3, 3)
         store_g(3, 2, 2)
-        gate_up(2, 4, "bank")
+        gate_up(2, 4, "hi")
         silu(2, 4)
         product(2, 4)
-        gate_up(3, 4, "bank")
+        gate_up(3, 4, "hi")
         silu(3, 4)
         product(3, 4)
-        gate_up(2, 5, "bank")
+        gate_up(2, 5, "lo")
         silu(2, 5)
         product(2, 5)
         store_g(2, 4, 2)
-        gate_up(3, 5, "bank")
+        gate_up(3, 5, "lo")
         silu(3, 5)
         product(3, 5)
         store_g(3, 4, 2)
-        gate_up(2, 6, "bank")
+        gate_up(2, 6, "hi")
         silu(2, 6)
         product(2, 6)
         store_g(2, 6, 1)
-        gate_up(3, 6, "bank")
+        gate_up(3, 6, "hi")
         silu(3, 6)
         product(3, 6)
         store_g(3, 6, 1)
-        gate_up(2, 7, "bank")
+        gate_up(2, 7, "lo")
         silu(2, 7)
         product(2, 7)
         store_g(2, 7, 1)
-        gate_up(3, 7, "bank", 0, BANK // 2)
+        gate_up(3, 7, "lo", 0, BANK // 2)
         silu(3, 7, 0, BANK // 2)
-        gate_up(3, 7, "bank", BANK // 2, BANK // 2)
+        gate_up(3, 7, "hi", BANK // 2, BANK // 2)
         product(3, 7, 0, BANK // 2)
         store_part(3, 7, 0, BANK // 2)
         silu(3, 7, BANK // 2, BANK // 2)

from contextlib import ExitStack

import concourse.mybir as mybir
from concourse.masks import make_identity

F32 = mybir.dt.float32
BF16 = mybir.dt.bfloat16
I32 = mybir.dt.int32
U32 = mybir.dt.uint32
U8 = mybir.dt.uint8
FP8X4 = mybir.dt.float8_e4m3fn_x4
ALU = mybir.AluOpType
ACT = mybir.ActivationFunctionType

P = 128
TILES = 4
D = 1024
M = 4096
K_PASS = 512
PASSES = D // K_PASS
BANK = 512
HALVES = D // BANK
CHUNKS = M // BANK
LOADS = (1, 1, 1, 1, 1, 1, 1, 1)
EPS = 1e-6

FLOPS = 2 * TILES * P * D * (D + 2 * M)


def tile_transformerblocktpu_pb_kernel(
    tc, attn, x, w_o_words, w_o_scales, rms2_scale, w_gate_words, w_gate_scales, w_up_words, w_up_scales, out_0, out_1
):
    nc = tc.nc
    with ExitStack() as ctx:
        ctx.enter_context(tc.manual_schedule())
        keep = ctx.enter_context(tc.tile_pool(name="keep", bufs=1))
        ring = ctx.enter_context(tc.tile_pool(name="ring", bufs=4))
        psum = ctx.enter_context(tc.psum_pool(name="psum", bufs=4))

        minus_half = keep.tile([P, 1], F32)
        table_warm = keep.tile([P, 1], F32)
        wo_planes = keep.tile([P, D], U8, align_bytes=64)
        w_planes = keep.tile([P, 2 * PASSES, M // 4], U8, align_bytes=64)
        gain_row = keep.tile([P, D], BF16)
        ones = keep.tile([P, P], BF16)
        ident = keep.tile([P, P], F32)
        nc.vector.memset(minus_half[:], -0.5)
        nc.scalar.activation(out=table_warm[:], in_=minus_half[:], func=ACT.Silu)
        nc.vector.memset(gain_row[:].bitcast(I32), 0)
        nc.vector.memset(wo_planes[:].bitcast(I32), 0)
        nc.vector.memset(w_planes[:].rearrange("p a c -> p (a c)").bitcast(I32), 0)
        nc.vector.memset(ones[:], 1.0)
        make_identity(nc, ident[:])

        attn_sb = [keep.tile([P, D], BF16, name="attn%d" % m) for m in range(TILES)]
        x_sb = [keep.tile([P, D], BF16, name="x%d" % m) for m in range(TILES)]
        wo_words = keep.tile([P, PASSES, D], U32, align_bytes=64)
        w_pieces = [
            [keep.tile([P, PASSES, n * BANK], U32, name="w%d_%d" % (w, i), align_bytes=64) for w in range(2)]
            for i, n in enumerate(LOADS)
        ]
        where = [(i, j) for i, n in enumerate(LOADS) for j in range(n)]

        def load_attn(m):
            nc.sync.dma_start(out=attn_sb[m][:], in_=attn[m])

        def load_x(m):
            nc.sync.dma_start(out=x_sb[m][:], in_=x[m])

        def load_gain():
            nc.sync.dma_start(out=gain_row[0:1, :], in_=rms2_scale.rearrange("(o d) -> o d", o=1))

        def load_wo_scales():
            for q4 in range(4):
                nc.sync.dma_start(
                    out=wo_planes[32 * q4 : 32 * q4 + 4 * PASSES, :].bitcast(I32),
                    in_=w_o_scales[:, 4 * q4 : 4 * q4 + 4, :].bitcast(I32),
                )

        def load_wo():
            nc.sync.dma_start(
                out=wo_words[:].bitcast(I32), in_=w_o_words.rearrange("g p n t -> p g (n t)").bitcast(I32)
            )

        def load_wo_half(n):
            cols = slice(n * BANK, (n + 1) * BANK)
            nc.sync.dma_start(
                out=wo_words[:, :, cols].bitcast(I32),
                in_=w_o_words.rearrange("g p n t -> p g (n t)").bitcast(I32)[:, :, cols],
            )

        def load_w_scales(first, count):
            for i in range(first, first + count):
                area, q4 = divmod(i, 4)
                scales = (w_gate_scales, w_up_scales)[area // PASSES]
                nc.sync.dma_start(
                    out=w_planes[32 * q4 : 32 * q4 + 16, area, :].bitcast(I32),
                    in_=scales[area % PASSES, 4 * q4 : 4 * q4 + 4, :].bitcast(I32).rearrange("r (s c) -> s r c", s=4),
                )

        def load_w(i):
            first = sum(LOADS[:i]) * BANK
            for w, words in enumerate((w_gate_words, w_up_words)):
                nc.sync.dma_start(
                    out=w_pieces[i][w][:].bitcast(I32),
                    in_=words.rearrange("g p n t -> p g (n t)").bitcast(I32)[:, :, first : first + LOADS[i] * BANK],
                )

        load_attn(0)
        load_attn(1)
        load_gain()
        load_attn(2)
        load_attn(3)
        load_wo_half(0)
        load_wo_scales()
        load_wo_half(1)
        load_x(0)
        load_x(1)
        load_w_scales(0, 4)
        load_x(2)
        load_w_scales(4, 4)
        load_x(3)
        load_w_scales(8, 4)
        load_w(0)
        load_w_scales(12, 4)
        load_w(1)
        load_w(2)
        load_w(3)
        load_w(4)
        load_w(5)
        load_w(6)
        load_w(7)

        a_codes = keep.tile([P, TILES, PASSES, P], U32, align_bytes=64)
        a_planes = keep.tile([P, TILES, PASSES, P], U8, align_bytes=64)
        h_codes = keep.tile([P, TILES, PASSES, P], U32, align_bytes=64)
        h_planes = keep.tile([P, TILES, PASSES, P], U8, align_bytes=64)
        gain_bc = keep.tile([P, D], BF16)
        x_mid = [keep.tile([P, D], F32, name="x_mid%d" % m) for m in range(TILES)]
        g_sb = [keep.tile([P, M], F32, name="g%d" % m) for m in range(TILES)]
        mean_sq = [keep.tile([P, HALVES], F32, name="mean_sq%d" % m) for m in range(TILES)]
        var = [keep.tile([P, 1], F32, name="var%d" % m) for m in range(TILES)]
        rstd = [keep.tile([P, 1], F32, name="rstd%d" % m) for m in range(TILES)]
        h_sb = [keep.tile([P, D], BF16, name="h%d" % m) for m in range(TILES)]
        flipped = {}
        grouped = {}
        spread = {}
        stage1_acc = {}
        stage2_acc = {}
        silu_sb = {}

        def flip(key, rows, first_pass, n_passes, banks):
            words = rows.bitcast(F32)
            turned = psum.tile([P, n_passes, 2, P], F32, tag=banks, name="turned")
            for g in range(n_passes):
                first_word = (K_PASS // 2) * (first_pass + g)
                for u in range(2):
                    nc.tensor.transpose(
                        turned[:, g, u, :], words[:, first_word + u : first_word + K_PASS // 2 : 2], ident[:]
                    )
            flipped[key] = turned

        def group(key, n_passes, tag):
            tile = ring.tile([P, n_passes * P * 4], BF16, align_bytes=64, tag=tag, name="tile")
            nc.scalar.copy(
                out=tile[:].bitcast(F32).rearrange("p (g r u) -> p g r u", g=n_passes, u=2),
                in_=flipped[key][:].rearrange("p g u r -> p g r u"),
            )
            grouped[key] = tile

        def flip_attn(m, banks):
            flip(("a", m), attn_sb[m][:], 0, PASSES, banks)

        def group_attn(m):
            group(("a", m), PASSES, "grouped_attn")

        def quantise_attn(m):
            nc.vector.quantize_mx(
                out=a_codes[:, m].rearrange("p g r -> p (g r)").bitcast(FP8X4),
                scales=a_planes[:, m].rearrange("p g r -> p (g r)"),
                in_=grouped[("a", m)][:],
            )

        def spread_gain(n, banks):
            acc = psum.tile([P, BANK], F32, tag=banks, name="acc0")
            nc.tensor.matmul(out=acc[:], lhsT=ones[:], rhs=gain_row[:, n * BANK : (n + 1) * BANK], start=True, stop=True)
            spread[n] = acc

        def keep_gain(n):
            nc.scalar.copy(out=gain_bc[:, n * BANK : (n + 1) * BANK], in_=spread[n][:])

        def keep_warm(spent):
            for i in range(2):
                nc.tensor.matmul(out=spent, lhsT=ones[:], rhs=gain_row[:, 0:BANK], start=True, stop=True)

        def stage1(m, n, banks):
            acc = psum.tile([P, BANK], F32, tag=banks, name="acc1")
            for g in range(PASSES):
                nc.tensor.matmul_mx(
                    out=acc[:],
                    lhsT=a_codes[:, m, g].bitcast(FP8X4),
                    lhsT_scale=a_planes[:, m, g],
                    rhs=wo_words[:, g, n * BANK : (n + 1) * BANK].bitcast(FP8X4),
                    rhs_scale=wo_planes[4 * g : P, n * BANK : (n + 1) * BANK],
                    start=(g == 0),
                    stop=(g == PASSES - 1),
                )
            stage1_acc[(m, n)] = acc

        def residual(m, n):
            cols = slice(n * BANK, (n + 1) * BANK)
            nc.vector.tensor_tensor(
                out=x_mid[m][:, cols], in0=stage1_acc[(m, n)][:], in1=x_sb[m][:, cols], op=ALU.add
            )

        def squares(m, n):
            junk = ring.tile([P, BANK], BF16, name="junk")
            nc.scalar.activation(
                out=junk[:], in_=x_mid[m][:, n * BANK : (n + 1) * BANK], func=ACT.Square, scale=1.0 / 32.0,
                accum_out=mean_sq[m][:, n : n + 1],
            )

        def store_x_mid(m):
            nc.sync.dma_start(out=out_0[m], in_=x_mid[m][:])

        def inverse_rms(m):
            nc.vector.scalar_tensor_tensor(
                out=var[m][:], in0=mean_sq[m][:, 0:1], scalar=EPS, in1=mean_sq[m][:, 1:2], op0=ALU.add, op1=ALU.add
            )
            nc.gpsimd.tensor_tensor(out=rstd[m][:], in0=var[m][:], in1=minus_half[:], op=ALU.pow)

        def normed(m, g):
            cols = slice(g * K_PASS, (g + 1) * K_PASS)
            nc.vector.scalar_tensor_tensor(
                out=h_sb[m][:, cols], in0=x_mid[m][:, cols], scalar=rstd[m][:, 0:1], in1=gain_bc[:, cols],
                op0=ALU.mult, op1=ALU.mult,
            )

        def flip_h(m, g, banks):
            flip(("h", m, g), h_sb[m][:], g, 1, banks)

        def group_h(m, g):
            group(("h", m, g), 1, "grouped_h")

        def quantise_h(m, g):
            nc.vector.quantize_mx(
                out=h_codes[:, m, g].bitcast(FP8X4), scales=h_planes[:, m, g], in_=grouped[("h", m, g)][:]
            )

        def gate_up(m, c, banks, first=0, width=BANK):
            accs = []
            for w in range(2):
                acc = psum.tile([P, width], F32, tag=banks, name="acc2")
                for g in range(PASSES):
                    nc.tensor.matmul_mx(
                        out=acc[:],
                        lhsT=h_codes[:, m, g].bitcast(FP8X4),
                        lhsT_scale=h_planes[:, m, g],
                        rhs=w_pieces[where[c][0]][w][
                            :, g, where[c][1] * BANK + first : where[c][1] * BANK + first + width
                        ].bitcast(FP8X4),
                        rhs_scale=w_planes[
                            4 * (c // 2) : P, PASSES * w + g, (c % 2) * BANK + first : (c % 2) * BANK + first + width
                        ],
                        start=(g == 0),
                        stop=(g == PASSES - 1),
                    )
                accs.append(acc)
            stage2_acc[(m, c, first)] = accs

        def silu(m, c, first=0, width=BANK):
            tile = ring.tile([P, width], F32, name="silu_tile")
            nc.scalar.activation(out=tile[:], in_=stage2_acc[(m, c, first)][0][:], func=ACT.Silu)
            silu_sb[(m, c, first)] = tile

        def product(m, c, first=0, width=BANK):
            nc.vector.tensor_tensor(
                out=g_sb[m][:, c * BANK + first : c * BANK + first + width], in0=silu_sb[(m, c, first)][:],
                in1=stage2_acc[(m, c, first)][1][:], op=ALU.mult,
            )

        def store_part(m, c, first, width):
            cols = slice(c * BANK + first, c * BANK + first + width)
            nc.sync.dma_start(out=out_1[m][:, cols], in_=g_sb[m][:, cols])

        def store_g(m, first_chunk, n_chunks):
            cols = slice(first_chunk * BANK, (first_chunk + n_chunks) * BANK)
            nc.sync.dma_start(out=out_1[m][:, cols], in_=g_sb[m][:, cols])

        flip_attn(0, "lo")
        group_attn(0)
        quantise_attn(0)
        flip_attn(1, "lo")
        group_attn(1)
        quantise_attn(1)
        flip_attn(2, "lo")
        group_attn(2)
        quantise_attn(2)
        flip_attn(3, "lo")
        group_attn(3)
        quantise_attn(3)
        spread_gain(0, "hi")
        keep_gain(0)
        spread_gain(1, "hi")
        keep_gain(1)
        stage1(0, 0, "lo")
        stage1(0, 1, "lo")
        stage1(1, 0, "lo")
        stage1(1, 1, "lo")
        stage1(2, 0, "hi")
        stage1(2, 1, "hi")
        stage1(3, 0, "hi")
        stage1(3, 1, "hi")
        residual(0, 0)
        squares(0, 0)
        residual(0, 1)
        squares(0, 1)
        store_x_mid(0)
        residual(1, 0)
        squares(1, 0)
        residual(1, 1)
        squares(1, 1)
        store_x_mid(1)
        inverse_rms(0)
        residual(2, 0)
        squares(2, 0)
        residual(2, 1)
        squares(2, 1)
        store_x_mid(2)
        inverse_rms(1)
        normed(0, 0)
        normed(0, 1)
        normed(1, 0)
        normed(1, 1)
        flip_h(0, 0, "lo")
        group_h(0, 0)
        flip_h(0, 1, "lo")
        group_h(0, 1)
        quantise_h(0, 0)
        quantise_h(0, 1)
        flip_h(1, 0, "lo")
        group_h(1, 0)
        flip_h(1, 1, "lo")
        group_h(1, 1)
        quantise_h(1, 0)
        quantise_h(1, 1)
        gate_up(0, 0, "lo")
        silu(0, 0)
        gate_up(1, 0, "lo")
        silu(1, 0)
        residual(3, 0)
        squares(3, 0)
        residual(3, 1)
        squares(3, 1)
        store_x_mid(3)
        inverse_rms(2)
        product(0, 0)
        inverse_rms(3)
        product(1, 0)
        gate_up(0, 1, "hi")
        silu(0, 1)
        product(0, 1)
        store_g(0, 0, 2)
        gate_up(1, 1, "hi")
        silu(1, 1)
        product(1, 1)
        store_g(1, 0, 2)
        gate_up(0, 2, "lo")
        silu(0, 2)
        product(0, 2)
        gate_up(1, 2, "lo")
        silu(1, 2)
        product(1, 2)
        normed(2, 0)
        normed(2, 1)
        normed(3, 0)
        normed(3, 1)
        gate_up(0, 3, "hi")
        silu(0, 3)
        product(0, 3)
        store_g(0, 2, 2)
        gate_up(1, 3, "hi")
        silu(1, 3)
        product(1, 3)
        store_g(1, 2, 2)
        gate_up(0, 4, "lo")
        silu(0, 4)
        product(0, 4)
        gate_up(1, 4, "lo")
        silu(1, 4)
        product(1, 4)
        flip_h(2, 0, "hi")
        group_h(2, 0)
        flip_h(2, 1, "hi")
        group_h(2, 1)
        flip_h(3, 0, "hi")
        group_h(3, 0)
        flip_h(3, 1, "hi")
        group_h(3, 1)
        gate_up(0, 5, "lo")
        silu(0, 5)
        product(0, 5)
        store_g(0, 4, 2)
        gate_up(1, 5, "lo")
        silu(1, 5)
        product(1, 5)
        store_g(1, 4, 2)
        quantise_h(2, 0)
        quantise_h(2, 1)
        quantise_h(3, 0)
        quantise_h(3, 1)
        gate_up(0, 6, "hi")
        silu(0, 6)
        product(0, 6)
        gate_up(1, 6, "hi")
        silu(1, 6)
        product(1, 6)
        gate_up(0, 7, "lo")
        silu(0, 7)
        product(0, 7)
        store_g(0, 6, 2)
        gate_up(1, 7, "lo")
        silu(1, 7)
        product(1, 7)
        store_g(1, 6, 2)
        gate_up(2, 0, "hi")
        silu(2, 0)
        product(2, 0)
        gate_up(3, 0, "hi")
        silu(3, 0)
        product(3, 0)
        gate_up(2, 1, "lo")
        silu(2, 1)
        product(2, 1)
        store_g(2, 0, 2)
        gate_up(3, 1, "lo")
        silu(3, 1)
        product(3, 1)
        store_g(3, 0, 2)
        gate_up(2, 2, "hi")
        silu(2, 2)
        product(2, 2)
        gate_up(3, 2, "hi")
        silu(3, 2)
        product(3, 2)
        gate_up(2, 3, "lo")
        silu(2, 3)
        product(2, 3)
        store_g(2, 2, 2)
        gate_up(3, 3, "lo")
        silu(3, 3)
        product(3, 3)
        store_g(3, 2, 2)
        gate_up(2, 4, "hi")
        silu(2, 4)
        product(2, 4)
        gate_up(3, 4, "hi")
        silu(3, 4)
        product(3, 4)
        gate_up(2, 5, "lo")
        silu(2, 5)
        product(2, 5)
        store_g(2, 4, 2)
        gate_up(3, 5, "lo")
        silu(3, 5)
        product(3, 5)
        store_g(3, 4, 2)
        gate_up(2, 6, "hi")
        silu(2, 6)
        product(2, 6)
        store_g(2, 6, 1)
        gate_up(3, 6, "hi")
        silu(3, 6)
        product(3, 6)
        store_g(3, 6, 1)
        gate_up(2, 7, "lo")
        silu(2, 7)
        product(2, 7)
        store_g(2, 7, 1)
        gate_up(3, 7, "lo", 0, BANK // 2)
        silu(3, 7, 0, BANK // 2)
        gate_up(3, 7, "hi", BANK // 2, BANK // 2)
        product(3, 7, 0, BANK // 2)
        store_part(3, 7, 0, BANK // 2)
        silu(3, 7, BANK // 2, BANK // 2)
        product(3, 7, BANK // 2, BANK // 2)
        store_part(3, 7, BANK // 2, BANK // 2)
